import numpy as np
import ml_dtypes


def mxq(x, axis, fmt="e4m3"):
    dtype, down = {"e4m3": (ml_dtypes.float8_e4m3fn, 7), "e5m2": (ml_dtypes.float8_e5m2, 14)}[fmt]
    v = np.moveaxis(np.asarray(x, np.float32).astype(ml_dtypes.bfloat16).astype(np.float64), axis, -1)
    blocks = v.reshape(v.shape[:-1] + (-1, 32))
    amax = np.abs(blocks).max(-1, keepdims=True)
    byte = np.maximum(np.where(amax > 0, np.frexp(amax)[1] - 1 + 127, 0) - down, 1)
    scale = np.exp2(byte - 127.0)
    codes = (blocks / scale).astype(np.float32).astype(dtype).astype(np.float64)
    return np.moveaxis((codes * scale).reshape(v.shape), -1, axis)


WIDE = False


def mx_kscale(k):
    if not WIDE:
        return np.ones(k)
    levels = np.array([20, -20, 10, -10, 0])
    a = np.random.permutation(np.resize(levels, k // 512 * 4)).reshape(k // 512, 4)
    idx = np.arange(k)
    return np.exp2(a[idx // 512, idx % 128 // 32])


BF16 = ml_dtypes.bfloat16


def bf(x):
    return np.asarray(x, np.float32).astype(BF16)


def f64(x):
    return np.asarray(x).astype(np.float64)


B, CIN, COUT, H, W = 4, 512, 512, 32, 32
T = B * H * W


def setup_inputs():
    s = mx_kscale(T).reshape(B, 1, H, W)
    x = np.random.standard_normal((B, CIN, H, W)) * s
    weight = np.random.uniform(-1.0, 1.0, (CIN, COUT)) * np.sqrt(3.0 / CIN)
    g = np.random.standard_normal((B, COUT, H, W)) * np.exp2(np.random.randint(-12, 1, (B, 1, H, W))) / s
    return {"x": bf(x), "weight": bf(weight), "grad_out": bf(g)}


def reference(x, weight, grad_out):
    xt = f64(x).transpose(1, 0, 2, 3).reshape(CIN, T)
    gt = f64(grad_out).transpose(1, 0, 2, 3).reshape(COUT, T)
    return mxq(xt, 1, "e4m3") @ mxq(gt, 1, "e5m2").T

@@ -1,0 +1,149 @@
+from contextlib import ExitStack
+
+import concourse.mybir as mybir
+from concourse.masks import make_identity
+
+FLOPS = 2 * 512 * 512 * 4096
+BYTES = 2 * (4 * 512 * 1024 * 2) + 512 * 512 * 4
+
+BF16 = mybir.dt.bfloat16
+F32 = mybir.dt.float32
+U32 = mybir.dt.uint32
+U8 = mybir.dt.uint8
+E4M3X4 = mybir.dt.float8_e4m3fn_x4
+E5M2X4 = mybir.dt.float8_e5m2_x4
+
+P = 128
+BATCH = 4
+SLOTS = 4
+PIX = 1024
+HALVES = 2
+
+
+def tile_simpleconvolution_kernel(tc, x, weight, grad_out, out):
+    nc = tc.nc
+    with ExitStack() as ctx:
+        const = ctx.enter_context(tc.tile_pool(name="const", bufs=1))
+        keep = ctx.enter_context(tc.tile_pool(name="keep", bufs=1))
+        tbanks = ctx.enter_context(tc.psum_pool(name="tbanks", bufs=4))
+        abanks = ctx.enter_context(tc.psum_pool(name="abanks", bufs=1))
+        ctx.enter_context(tc.manual_schedule())
+
+        dram = {"x": x, "g": grad_out}
+        fmt = {"x": E4M3X4, "g": E5M2X4}
+        src = {}
+        raw = {}
+        grp = {}
+        codes = {}
+        scales = {}
+        for op in ("g", "x"):
+            for b in range(BATCH):
+                key = (op, b)
+                src[key] = dram[op][b].rearrange("(p t) h w -> p (t h w)", t=SLOTS)
+                raw[key] = keep.tile([P, SLOTS * PIX], BF16, name="raw_%s%d" % key)
+                grp[key] = keep.tile([P, SLOTS * PIX], BF16, name="grp_%s%d" % key, align_bytes=64)
+                codes[key] = keep.tile([P, PIX], U32, name="codes_%s%d" % key, align_bytes=64)
+                scales[key] = keep.tile([P, PIX], U8, name="scales_%s%d" % key, align_bytes=64)
+        acc = [abanks.tile([P, 512], F32, name="acc%d" % t) for t in range(SLOTS)]
+        res = keep.tile([P, SLOTS * 512], F32, name="res")
+        out_v = out.rearrange("(p t) o -> p t o", t=SLOTS)
+
+        def load(op, b, pieces):
+            width = SLOTS * PIX // pieces
+            for i in range(pieces):
+                cols = slice(i * width, (i + 1) * width)
+                nc.sync.dma_start(out=raw[(op, b)][:, cols], in_=src[(op, b)][:, cols])
+
+        load("g", 0, 4)
+        load("x", 0, 4)
+        for b in range(1, BATCH):
+            load("g", b, 1)
+            load("x", b, 2)
+
+        ident = const.tile([P, P], F32, name="ident")
+        make_identity(nc, ident[:])
+
+        def transposes(op, b, slots, engines):
+            words = raw[(op, b)][:].bitcast(F32)
+            grouped = grp[(op, b)][:].bitcast(F32)
+            for t, eng in zip(slots, engines):
+                bank = tbanks.tile([P, 512], F32, name="bank")
+                for j in range(4):
+                    nc.tensor.transpose(
+                        out=bank[:, j * P : (j + 1) * P],
+                        in_=words[:, t * 512 + j * P : t * 512 + (j + 1) * P],
+                        identity=ident[:],
+                    )
+                planes = bank[:].rearrange("q (g u p) -> q g p u", g=HALVES, u=2)
+                if op == "x":
+                    dst = grouped[:, t * 512 : (t + 1) * 512].rearrange("q (g p u) -> q g p u", g=HALVES, u=2)
+                else:
+                    dst = grouped.rearrange("q (g t p u) -> q g t p u", g=HALVES, t=SLOTS, u=2)[:, :, t, :, :]
+                if eng == "s":
+                    nc.scalar.copy(out=dst, in_=planes)
+                else:
+                    nc.vector.tensor_copy(out=dst, in_=planes)
+
+        def quantise(op, b, piece):
+            key = (op, b)
+            nc.vector.quantize_mx(
+                out=codes[key][:, piece * 512 : (piece + 1) * 512].bitcast(fmt[op]),
+                scales=scales[key][:, piece * 512 : (piece + 1) * 512],
+                in_=grp[key][:, piece * 2048 : (piece + 1) * 2048],
+            )
+
+        done = [0] * SLOTS
+
+        def passes(b, pairs):
+            for g, t in pairs:
+                xc = slice(t * 256 + g * P, t * 256 + (g + 1) * P)
+                gc = slice(g * 512, (g + 1) * 512)
+                nc.tensor.matmul_mx(
+                    out=acc[t][:],
+                    lhsT=codes[("x", b)][:, xc].bitcast(E4M3X4),
+                    lhsT_scale=scales[("x", b)][:, xc],
+                    rhs=codes[("g", b)][:, gc].bitcast(E5M2X4),
+                    rhs_scale=scales[("g", b)][:, gc],
+                    start=(done[t] == 0),
+                    stop=(done[t] == BATCH * HALVES - 1),
+                )
+                done[t] += 1
+
+        def whole(op, b):
+            transposes(op, b, (0, 1, 2, 3), "sssv")
+            quantise(op, b, 0)
+            quantise(op, b, 1)
+
+        def half(g):
+            return [(g, t) for t in range(SLOTS)]
+
+        whole("g", 0)
+        whole("x", 0)
+        passes(0, half(0))
+        whole("g", 1)
+        passes(0, half(1))
+        whole("x", 1)
+        whole("g", 2)
+        passes(1, half(0))
+        whole("x", 2)
+        passes(1, half(1))
+        whole("g", 3)
+        passes(2, half(0))
+        transposes("x", 3, (0, 1), "sv")
+        quantise("x", 3, 0)
+        passes(2, half(1))
+        transposes("x", 3, (2, 3), "sv")
+        quantise("x", 3, 1)
+
+        def finish(t, eng):
+            dst = res[:, t * 512 : (t + 1) * 512]
+            spread = acc[t][:].rearrange("q (t p) -> q p t", t=SLOTS)
+            if eng == "s":
+                nc.scalar.copy(out=dst.rearrange("q (p t) -> q p t", t=SLOTS), in_=spread)
+            else:
+                nc.vector.tensor_copy(out=dst.rearrange("q (p t) -> q p t", t=SLOTS), in_=spread)
+            nc.sync.dma_start(out=out_v[:, t, :], in_=dst)
+
+        for t, eng in zip(range(SLOTS), "svsv"):
+            passes(3, [(0, t), (1, t)])
+            finish(t, eng)

@@ -63,6 +63,15 @@ def tile_simpleconvolution_kernel(tc, x, weight, grad_out, out):
         ident = const.tile([P, P], F32, name="ident")
         make_identity(nc, ident[:])
 
+        warm = const.tile([P, 512], BF16, name="warm")
+        nc.vector.memset(warm[:], 0.0)
+
+        def dummies(n):
+            for i in range(n):
+                nc.tensor.matmul(out=acc[3][:], lhsT=warm[:, 0:P], rhs=warm[:], start=True, stop=True)
+
+        dummies(4)
+
         def transposes(op, b, slots, engines):
             words = raw[(op, b)][:].bitcast(F32)
             grouped = grp[(op, b)][:].bitcast(F32)
@@ -83,6 +92,8 @@ def tile_simpleconvolution_kernel(tc, x, weight, grad_out, out):
                     nc.scalar.copy(out=dst, in_=planes)
                 else:
                     nc.vector.tensor_copy(out=dst, in_=planes)
+                if b == 0:
+                    dummies(1)
 
         def quantise(op, b, piece):
             key = (op, b)

@@ -92,15 +92,16 @@ def tile_simpleconvolution_kernel(tc, x, weight, grad_out, out):
                     nc.scalar.copy(out=dst, in_=planes)
                 else:
                     nc.vector.tensor_copy(out=dst, in_=planes)
-                if b == 0:
+                if b == 0 and (op, t) != ("x", SLOTS - 1):
                     dummies(1)
 
-        def quantise(op, b, piece):
+        def quantise(op, b, first, count):
             key = (op, b)
+            cols = slice(first * P, (first + count) * P)
             nc.vector.quantize_mx(
-                out=codes[key][:, piece * 512 : (piece + 1) * 512].bitcast(fmt[op]),
-                scales=scales[key][:, piece * 512 : (piece + 1) * 512],
-                in_=grp[key][:, piece * 2048 : (piece + 1) * 2048],
+                out=codes[key][:, cols].bitcast(fmt[op]),
+                scales=scales[key][:, cols],
+                in_=grp[key][:, first * 512 : (first + count) * 512],
             )
 
         done = [0] * SLOTS
@@ -121,30 +122,32 @@ def tile_simpleconvolution_kernel(tc, x, weight, grad_out, out):
                 done[t] += 1
 
         def whole(op, b):
-            transposes(op, b, (0, 1, 2, 3), "sssv")
-            quantise(op, b, 0)
-            quantise(op, b, 1)
+            transposes(op, b, (0, 1, 2, 3), "ssvs")
+            quantise(op, b, 0, 4)
+            quantise(op, b, 4, 4)
 
-        def half(g):
-            return [(g, t) for t in range(SLOTS)]
+        def pair(t0):
+            return [(g, t) for t in (t0, t0 + 1) for g in range(HALVES)]
 
-        whole("g", 0)
-        whole("x", 0)
-        passes(0, half(0))
+        for t in range(SLOTS):
+            transposes("g", 0, (t,), "s")
+            quantise("g", 0, t, 1)
+            quantise("g", 0, SLOTS + t, 1)
+        for t in range(SLOTS):
+            transposes("x", 0, (t,), "s")
+            quantise("x", 0, 2 * t, 2)
+        passes(0, pair(0))
         whole("g", 1)
-        passes(0, half(1))
         whole("x", 1)
+        passes(0, pair(2))
         whole("g", 2)
-        passes(1, half(0))
         whole("x", 2)
-        passes(1, half(1))
+        passes(1, pair(0))
+        passes(1, pair(2))
         whole("g", 3)
-        passes(2, half(0))
-        transposes("x", 3, (0, 1), "sv")
-        quantise("x", 3, 0)
-        passes(2, half(1))
-        transposes("x", 3, (2, 3), "sv")
-        quantise("x", 3, 1)
+        whole("x", 3)
+        passes(2, pair(0))
+        passes(2, pair(2))
 
         def finish(t, eng):
             dst = res[:, t * 512 : (t + 1) * 512]

@@ -72,10 +72,19 @@ def tile_simpleconvolution_kernel(tc, x, weight, grad_out, out):
 
         dummies(4)
 
-        def transposes(op, b, slots, engines):
+        def quantise(op, b, first, count):
+            key = (op, b)
+            cols = slice(first * P, (first + count) * P)
+            nc.vector.quantize_mx(
+                out=codes[key][:, cols].bitcast(fmt[op]),
+                scales=scales[key][:, cols],
+                in_=grp[key][:, first * 512 : (first + count) * 512],
+            )
+
+        def prepare(op, b):
             words = raw[(op, b)][:].bitcast(F32)
             grouped = grp[(op, b)][:].bitcast(F32)
-            for t, eng in zip(slots, engines):
+            for t in range(SLOTS):
                 bank = tbanks.tile([P, 512], F32, name="bank")
                 for j in range(4):
                     nc.tensor.transpose(
@@ -88,76 +97,54 @@ def tile_simpleconvolution_kernel(tc, x, weight, grad_out, out):
                     dst = grouped[:, t * 512 : (t + 1) * 512].rearrange("q (g p u) -> q g p u", g=HALVES, u=2)
                 else:
                     dst = grouped.rearrange("q (g t p u) -> q g t p u", g=HALVES, t=SLOTS, u=2)[:, :, t, :, :]
-                if eng == "s":
+                if t < SLOTS - 1:
                     nc.scalar.copy(out=dst, in_=planes)
                 else:
                     nc.vector.tensor_copy(out=dst, in_=planes)
                 if b == 0 and (op, t) != ("x", SLOTS - 1):
                     dummies(1)
+                if op == "x":
+                    quantise(op, b, HALVES * t, HALVES)
+                else:
+                    for g in range(HALVES):
+                        quantise(op, b, SLOTS * g + t, 1)
 
-        def quantise(op, b, first, count):
-            key = (op, b)
-            cols = slice(first * P, (first + count) * P)
-            nc.vector.quantize_mx(
-                out=codes[key][:, cols].bitcast(fmt[op]),
-                scales=scales[key][:, cols],
-                in_=grp[key][:, first * 512 : (first + count) * 512],
-            )
+        def multiply(b, slots):
+            for t in slots:
+                for g in range(HALVES):
+                    xc = slice((HALVES * t + g) * P, (HALVES * t + g + 1) * P)
+                    gc = slice(g * 512, (g + 1) * 512)
+                    nc.tensor.matmul_mx(
+                        out=acc[t][:],
+                        lhsT=codes[("x", b)][:, xc].bitcast(E4M3X4),
+                        lhsT_scale=scales[("x", b)][:, xc],
+                        rhs=codes[("g", b)][:, gc].bitcast(E5M2X4),
+                        rhs_scale=scales[("g", b)][:, gc],
+                        start=(b == 0 and g == 0),
+                        stop=(b == BATCH - 1 and g == HALVES - 1),
+                    )
 
-        done = [0] * SLOTS
-
-        def passes(b, pairs):
-            for g, t in pairs:
-                xc = slice(t * 256 + g * P, t * 256 + (g + 1) * P)
-                gc = slice(g * 512, (g + 1) * 512)
-                nc.tensor.matmul_mx(
-                    out=acc[t][:],
-                    lhsT=codes[("x", b)][:, xc].bitcast(E4M3X4),
-                    lhsT_scale=scales[("x", b)][:, xc],
-                    rhs=codes[("g", b)][:, gc].bitcast(E5M2X4),
-                    rhs_scale=scales[("g", b)][:, gc],
-                    start=(done[t] == 0),
-                    stop=(done[t] == BATCH * HALVES - 1),
-                )
-                done[t] += 1
-
-        def whole(op, b):
-            transposes(op, b, (0, 1, 2, 3), "ssvs")
-            quantise(op, b, 0, 4)
-            quantise(op, b, 4, 4)
-
-        def pair(t0):
-            return [(g, t) for t in (t0, t0 + 1) for g in range(HALVES)]
-
-        for t in range(SLOTS):
-            transposes("g", 0, (t,), "s")
-            quantise("g", 0, t, 1)
-            quantise("g", 0, SLOTS + t, 1)
-        for t in range(SLOTS):
-            transposes("x", 0, (t,), "s")
-            quantise("x", 0, 2 * t, 2)
-        passes(0, pair(0))
-        whole("g", 1)
-        whole("x", 1)
-        passes(0, pair(2))
-        whole("g", 2)
-        whole("x", 2)
-        passes(1, pair(0))
-        passes(1, pair(2))
-        whole("g", 3)
-        whole("x", 3)
-        passes(2, pair(0))
-        passes(2, pair(2))
-
-        def finish(t, eng):
+        def finish(t):
             dst = res[:, t * 512 : (t + 1) * 512]
             spread = acc[t][:].rearrange("q (t p) -> q p t", t=SLOTS)
-            if eng == "s":
+            if t % 2 == 0:
                 nc.scalar.copy(out=dst.rearrange("q (p t) -> q p t", t=SLOTS), in_=spread)
             else:
                 nc.vector.tensor_copy(out=dst.rearrange("q (p t) -> q p t", t=SLOTS), in_=spread)
             nc.sync.dma_start(out=out_v[:, t, :], in_=dst)
 
-        for t, eng in zip(range(SLOTS), "svsv"):
-            passes(3, [(0, t), (1, t)])
-            finish(t, eng)
+        prepare("g", 0)
+        prepare("x", 0)
+        multiply(0, (0, 1))
+        prepare("g", 1)
+        multiply(0, (2,))
+        prepare("x", 1)
+        multiply(0, (3,))
+        for b in range(1, BATCH - 1):
+            prepare("g", b + 1)
+            multiply(b, (0, 1))
+            prepare("x", b + 1)
+            multiply(b, (2, 3))
+        for t in range(SLOTS):
+            multiply(BATCH - 1, (t,))
+            finish(t)

@@ -103,11 +103,11 @@ def tile_simpleconvolution_kernel(tc, x, weight, grad_out, out):
                     nc.vector.tensor_copy(out=dst, in_=planes)
                 if b == 0 and (op, t) != ("x", SLOTS - 1):
                     dummies(1)
-                if op == "x":
-                    quantise(op, b, HALVES * t, HALVES)
-                else:
-                    for g in range(HALVES):
-                        quantise(op, b, SLOTS * g + t, 1)
+                if op == "x" and t % 2 == 1:
+                    quantise(op, b, HALVES * (t - 1), 4)
+            if op == "g":
+                for g in range(HALVES):
+                    quantise(op, b, SLOTS * g, 4)
 
         def multiply(b, slots):
             for t in slots:

@@ -54,34 +54,26 @@ def tile_simpleconvolution_kernel(tc, x, weight, grad_out, out):
                 cols = slice(i * width, (i + 1) * width)
                 nc.sync.dma_start(out=raw[(op, b)][:, cols], in_=src[(op, b)][:, cols])
 
-        load("g", 0, 4)
-        load("x", 0, 4)
-        for b in range(1, BATCH):
-            load("g", b, 1)
-            load("x", b, 2)
+        for b in range(BATCH):
+            load("g", b, 4 if b == 0 else 2)
+            load("x", b, 4 if b == 0 else 2)
 
         ident = const.tile([P, P], F32, name="ident")
         make_identity(nc, ident[:])
 
-        warm = const.tile([P, 512], BF16, name="warm")
-        nc.vector.memset(warm[:], 0.0)
-
         def dummies(n):
             for i in range(n):
-                nc.tensor.matmul(out=acc[3][:], lhsT=warm[:, 0:P], rhs=warm[:], start=True, stop=True)
+                nc.tensor.matmul(out=acc[3][:, 0:P], lhsT=ident[:], rhs=ident[:], start=True, stop=True)
 
-        dummies(4)
-
-        def quantise(op, b, first, count):
+        def quantise(op, b, half):
             key = (op, b)
-            cols = slice(first * P, (first + count) * P)
             nc.vector.quantize_mx(
-                out=codes[key][:, cols].bitcast(fmt[op]),
-                scales=scales[key][:, cols],
-                in_=grp[key][:, first * 512 : (first + count) * 512],
+                out=codes[key][:, half * 512 : (half + 1) * 512].bitcast(fmt[op]),
+                scales=scales[key][:, half * 512 : (half + 1) * 512],
+                in_=grp[key][:, half * 2048 : (half + 1) * 2048],
             )
 
-        def prepare(op, b):
+        def prepare(op, b, keep_clock):
             words = raw[(op, b)][:].bitcast(F32)
             grouped = grp[(op, b)][:].bitcast(F32)
             for t in range(SLOTS):
@@ -101,28 +93,24 @@ def tile_simpleconvolution_kernel(tc, x, weight, grad_out, out):
                     nc.scalar.copy(out=dst, in_=planes)
                 else:
                     nc.vector.tensor_copy(out=dst, in_=planes)
-                if b == 0 and (op, t) != ("x", SLOTS - 1):
+                if keep_clock:
                     dummies(1)
-                if op == "x" and t % 2 == 1:
-                    quantise(op, b, HALVES * (t - 1), 4)
-            if op == "g":
-                for g in range(HALVES):
-                    quantise(op, b, SLOTS * g, 4)
+            quantise(op, b, 0)
+            quantise(op, b, 1)
 
-        def multiply(b, slots):
-            for t in slots:
-                for g in range(HALVES):
-                    xc = slice((HALVES * t + g) * P, (HALVES * t + g + 1) * P)
-                    gc = slice(g * 512, (g + 1) * 512)
-                    nc.tensor.matmul_mx(
-                        out=acc[t][:],
-                        lhsT=codes[("x", b)][:, xc].bitcast(E4M3X4),
-                        lhsT_scale=scales[("x", b)][:, xc],
-                        rhs=codes[("g", b)][:, gc].bitcast(E5M2X4),
-                        rhs_scale=scales[("g", b)][:, gc],
-                        start=(b == 0 and g == 0),
-                        stop=(b == BATCH - 1 and g == HALVES - 1),
-                    )
+        def multiply(b, pairs):
+            for g, t in pairs:
+                xc = slice((HALVES * t + g) * P, (HALVES * t + g + 1) * P)
+                gc = slice(g * 512, (g + 1) * 512)
+                nc.tensor.matmul_mx(
+                    out=acc[t][:],
+                    lhsT=codes[("x", b)][:, xc].bitcast(E4M3X4),
+                    lhsT_scale=scales[("x", b)][:, xc],
+                    rhs=codes[("g", b)][:, gc].bitcast(E5M2X4),
+                    rhs_scale=scales[("g", b)][:, gc],
+                    start=(b == 0 and g == 0),
+                    stop=(b == BATCH - 1 and g == HALVES - 1),
+                )
 
         def finish(t):
             dst = res[:, t * 512 : (t + 1) * 512]
@@ -133,18 +121,16 @@ def tile_simpleconvolution_kernel(tc, x, weight, grad_out, out):
                 nc.vector.tensor_copy(out=dst.rearrange("q (p t) -> q p t", t=SLOTS), in_=spread)
             nc.sync.dma_start(out=out_v[:, t, :], in_=dst)
 
-        prepare("g", 0)
-        prepare("x", 0)
-        multiply(0, (0, 1))
-        prepare("g", 1)
-        multiply(0, (2,))
-        prepare("x", 1)
-        multiply(0, (3,))
-        for b in range(1, BATCH - 1):
-            prepare("g", b + 1)
-            multiply(b, (0, 1))
-            prepare("x", b + 1)
-            multiply(b, (2, 3))
+        dummies(5)
+        prepare("g", 0, True)
+        prepare("x", 0, True)
+        prepare("g", 1, True)
+        for b in range(BATCH - 1):
+            multiply(b, [(0, t) for t in range(SLOTS)])
+            prepare("x", b + 1, False)
+            multiply(b, [(1, t) for t in range(SLOTS)])
+            if b + 2 < BATCH:
+                prepare("g", b + 2, False)
         for t in range(SLOTS):
-            multiply(BATCH - 1, (t,))
+            multiply(BATCH - 1, [(g, t) for g in range(HALVES)])
             finish(t)

@@ -65,12 +65,12 @@ def tile_simpleconvolution_kernel(tc, x, weight, grad_out, out):
             for i in range(n):
                 nc.tensor.matmul(out=acc[3][:, 0:P], lhsT=ident[:], rhs=ident[:], start=True, stop=True)
 
-        def quantise(op, b, half):
+        def quantise(op, b, first, width):
             key = (op, b)
             nc.vector.quantize_mx(
-                out=codes[key][:, half * 512 : (half + 1) * 512].bitcast(fmt[op]),
-                scales=scales[key][:, half * 512 : (half + 1) * 512],
-                in_=grp[key][:, half * 2048 : (half + 1) * 2048],
+                out=codes[key][:, first : first + width].bitcast(fmt[op]),
+                scales=scales[key][:, first : first + width],
+                in_=grp[key][:, 4 * first : 4 * (first + width)],
             )
 
         def prepare(op, b, keep_clock):
@@ -89,14 +89,15 @@ def tile_simpleconvolution_kernel(tc, x, weight, grad_out, out):
                     dst = grouped[:, t * 512 : (t + 1) * 512].rearrange("q (g p u) -> q g p u", g=HALVES, u=2)
                 else:
                     dst = grouped.rearrange("q (g t p u) -> q g t p u", g=HALVES, t=SLOTS, u=2)[:, :, t, :, :]
-                if t < SLOTS - 1:
+                if t < SLOTS - 1 or (op, b) == ("x", BATCH - 1):
                     nc.scalar.copy(out=dst, in_=planes)
                 else:
                     nc.vector.tensor_copy(out=dst, in_=planes)
-                if keep_clock:
+                if t < keep_clock:
                     dummies(1)
-            quantise(op, b, 0)
-            quantise(op, b, 1)
+            calls = SLOTS if (op, b) == ("x", BATCH - 1) else HALVES
+            for i in range(calls):
+                quantise(op, b, i * PIX // calls, PIX // calls)
 
         def multiply(b, pairs):
             for g, t in pairs:
@@ -122,15 +123,15 @@ def tile_simpleconvolution_kernel(tc, x, weight, grad_out, out):
             nc.sync.dma_start(out=out_v[:, t, :], in_=dst)
 
         dummies(5)
-        prepare("g", 0, True)
-        prepare("x", 0, True)
-        prepare("g", 1, True)
+        prepare("g", 0, SLOTS)
+        prepare("x", 0, SLOTS)
+        prepare("g", 1, SLOTS - 1)
         for b in range(BATCH - 1):
             multiply(b, [(0, t) for t in range(SLOTS)])
-            prepare("x", b + 1, False)
+            prepare("x", b + 1, 0)
             multiply(b, [(1, t) for t in range(SLOTS)])
             if b + 2 < BATCH:
-                prepare("g", b + 2, False)
+                prepare("g", b + 2, 0)
         for t in range(SLOTS):
             multiply(BATCH - 1, [(g, t) for g in range(HALVES)])
             finish(t)

from contextlib import ExitStack

import concourse.mybir as mybir
from concourse.masks import make_identity

FLOPS = 2 * 512 * 512 * 4096
BYTES = 2 * (4 * 512 * 1024 * 2) + 512 * 512 * 4

BF16 = mybir.dt.bfloat16
F32 = mybir.dt.float32
U32 = mybir.dt.uint32
U8 = mybir.dt.uint8
E4M3X4 = mybir.dt.float8_e4m3fn_x4
E5M2X4 = mybir.dt.float8_e5m2_x4

P = 128
BATCH = 4
SLOTS = 4
PIX = 1024
HALVES = 2


def tile_simpleconvolution_kernel(tc, x, weight, grad_out, out):
    nc = tc.nc
    with ExitStack() as ctx:
        const = ctx.enter_context(tc.tile_pool(name="const", bufs=1))
        keep = ctx.enter_context(tc.tile_pool(name="keep", bufs=1))
        tbanks = ctx.enter_context(tc.psum_pool(name="tbanks", bufs=4))
        abanks = ctx.enter_context(tc.psum_pool(name="abanks", bufs=1))
        ctx.enter_context(tc.manual_schedule())

        dram = {"x": x, "g": grad_out}
        fmt = {"x": E4M3X4, "g": E5M2X4}
        src = {}
        raw = {}
        grp = {}
        codes = {}
        scales = {}
        for op in ("g", "x"):
            for b in range(BATCH):
                key = (op, b)
                src[key] = dram[op][b].rearrange("(p t) h w -> p (t h w)", t=SLOTS)
                raw[key] = keep.tile([P, SLOTS * PIX], BF16, name="raw_%s%d" % key)
                grp[key] = keep.tile([P, SLOTS * PIX], BF16, name="grp_%s%d" % key, align_bytes=64)
                codes[key] = keep.tile([P, PIX], U32, name="codes_%s%d" % key, align_bytes=64)
                scales[key] = keep.tile([P, PIX], U8, name="scales_%s%d" % key, align_bytes=64)
        acc = [abanks.tile([P, 512], F32, name="acc%d" % t) for t in range(SLOTS)]
        res = keep.tile([P, SLOTS * 512], F32, name="res")
        out_v = out.rearrange("(p t) o -> p t o", t=SLOTS)

        def load(op, b, pieces):
            width = SLOTS * PIX // pieces
            for i in range(pieces):
                cols = slice(i * width, (i + 1) * width)
                nc.sync.dma_start(out=raw[(op, b)][:, cols], in_=src[(op, b)][:, cols])

        for b in range(BATCH):
            load("g", b, 4 if b == 0 else 2)
            load("x", b, 4 if b == 0 else 2)

        ident = const.tile([P, P], F32, name="ident")
        make_identity(nc, ident[:])

        def dummies(n):
            for i in range(n):
                nc.tensor.matmul(out=acc[3][:, 0:P], lhsT=ident[:], rhs=ident[:], start=True, stop=True)

        def quantise(op, b, first, width):
            key = (op, b)
            nc.vector.quantize_mx(
                out=codes[key][:, first : first + width].bitcast(fmt[op]),
                scales=scales[key][:, first : first + width],
                in_=grp[key][:, 4 * first : 4 * (first + width)],
            )

        def prepare(op, b, keep_clock):
            words = raw[(op, b)][:].bitcast(F32)
            grouped = grp[(op, b)][:].bitcast(F32)
            for t in range(SLOTS):
                bank = tbanks.tile([P, 512], F32, name="bank")
                for j in range(4):
                    nc.tensor.transpose(
                        out=bank[:, j * P : (j + 1) * P],
                        in_=words[:, t * 512 + j * P : t * 512 + (j + 1) * P],
                        identity=ident[:],
                    )
                planes = bank[:].rearrange("q (g u p) -> q g p u", g=HALVES, u=2)
                if op == "x":
                    dst = grouped[:, t * 512 : (t + 1) * 512].rearrange("q (g p u) -> q g p u", g=HALVES, u=2)
                else:
                    dst = grouped.rearrange("q (g t p u) -> q g t p u", g=HALVES, t=SLOTS, u=2)[:, :, t, :, :]
                if t < SLOTS - 1 or (op, b) == ("x", BATCH - 1):
                    nc.scalar.copy(out=dst, in_=planes)
                else:
                    nc.vector.tensor_copy(out=dst, in_=planes)
                if t < keep_clock:
                    dummies(1)
            calls = SLOTS if (op, b) == ("x", BATCH - 1) else HALVES
            for i in range(calls):
                quantise(op, b, i * PIX // calls, PIX // calls)

        def multiply(b, pairs):
            for g, t in pairs:
                xc = slice((HALVES * t + g) * P, (HALVES * t + g + 1) * P)
                gc = slice(g * 512, (g + 1) * 512)
                nc.tensor.matmul_mx(
                    out=acc[t][:],
                    lhsT=codes[("x", b)][:, xc].bitcast(E4M3X4),
                    lhsT_scale=scales[("x", b)][:, xc],
                    rhs=codes[("g", b)][:, gc].bitcast(E5M2X4),
                    rhs_scale=scales[("g", b)][:, gc],
                    start=(b == 0 and g == 0),
                    stop=(b == BATCH - 1 and g == HALVES - 1),
                )

        def finish(t):
            dst = res[:, t * 512 : (t + 1) * 512]
            spread = acc[t][:].rearrange("q (t p) -> q p t", t=SLOTS)
            if t % 2 == 0:
                nc.scalar.copy(out=dst.rearrange("q (p t) -> q p t", t=SLOTS), in_=spread)
            else:
                nc.vector.tensor_copy(out=dst.rearrange("q (p t) -> q p t", t=SLOTS), in_=spread)
            nc.sync.dma_start(out=out_v[:, t, :], in_=dst)

        dummies(5)
        prepare("g", 0, SLOTS)
        prepare("x", 0, SLOTS)
        prepare("g", 1, SLOTS - 1)
        for b in range(BATCH - 1):
            multiply(b, [(0, t) for t in range(SLOTS)])
            prepare("x", b + 1, 0)
            multiply(b, [(1, t) for t in range(SLOTS)])
            if b + 2 < BATCH:
                prepare("g", b + 2, 0)
        for t in range(SLOTS):
            multiply(BATCH - 1, [(g, t) for g in range(HALVES)])
            finish(t)
